import numpy as np
import ml_dtypes


def mxq(x, axis, fmt="e4m3"):
    dtype, down = {"e4m3": (ml_dtypes.float8_e4m3fn, 7), "e5m2": (ml_dtypes.float8_e5m2, 14)}[fmt]
    v = np.moveaxis(np.asarray(x, np.float32).astype(ml_dtypes.bfloat16).astype(np.float64), axis, -1)
    blocks = v.reshape(v.shape[:-1] + (-1, 32))
    amax = np.abs(blocks).max(-1, keepdims=True)
    byte = np.maximum(np.where(amax > 0, np.frexp(amax)[1] - 1 + 127, 0) - down, 1)
    scale = np.exp2(byte - 127.0)
    codes = (blocks / scale).astype(np.float32).astype(dtype).astype(np.float64)
    return np.moveaxis((codes * scale).reshape(v.shape), -1, axis)


WIDE = False


def mx_kscale(k):
    if not WIDE:
        return np.ones(k)
    levels = np.array([10, -10, 5, -5, 0])
    a = np.random.permutation(np.resize(levels, k // 512 * 4)).reshape(k // 512, 4)
    idx = np.arange(k)
    return np.exp2(a[idx // 512, idx % 128 // 32])


BF16 = ml_dtypes.bfloat16


def bf(x):
    return np.asarray(x, np.float32).astype(BF16)


def f64(x):
    return np.asarray(x).astype(np.float64)


B, HH, WW, E, NH, D = 1, 1024, 8, 1024, 2, 128
KD = NH * D


def setup_inputs():
    s = mx_kscale(E)
    return {"x": bf(np.random.standard_normal((B, HH, WW, E)) * s),
            "Wk": bf(np.random.standard_normal((KD, E)) * 0.2 / np.sqrt(E) / s),
            "bk": bf(np.random.standard_normal(KD) * 0.05),
            "Wv": bf(np.random.standard_normal((KD, E)) * 0.2 / np.sqrt(E) / s),
            "bv": bf(np.random.standard_normal(KD) * 0.25 / np.sqrt(HH))}


def reference(x, Wk, bk, Wv, bv):
    xq = mxq(f64(x), 3, "e4m3")
    k = np.maximum((xq @ mxq(f64(Wk).T, 0, "e4m3")) + f64(bk), 0.0).reshape(B, HH, WW * NH, D)
    v = ((xq @ mxq(f64(Wv).T, 0, "e4m3")) + f64(bv)).reshape(B, HH, WW * NH, D)
    kv = mxq(k.transpose(0, 2, 3, 1), 3, "e4m3") @ mxq(v.transpose(0, 2, 1, 3), 2, "e4m3")
    return kv.reshape(B, WW, NH, D, D)

@@ -1,0 +1,195 @@
+from contextlib import ExitStack
+
+import concourse.mybir as mybir
+from concourse.masks import make_identity
+
+BF16 = mybir.dt.bfloat16
+F32 = mybir.dt.float32
+U32 = mybir.dt.uint32
+U8 = mybir.dt.uint8
+FP8X4 = mybir.dt.float8_e4m3fn_x4
+
+P = 128
+PACK = 4
+K_PASS = P * PACK
+
+HEIGHT = 1024
+WIDTH = 8
+CHANNELS = 1024
+HEADS = 2
+HEAD_DIM = 128
+
+ROW_TILES = 4
+CHANNEL_PASSES = CHANNELS // K_PASS
+HEIGHT_PASSES = HEIGHT // K_PASS
+SLABS = WIDTH * HEIGHT_PASSES
+OUT_BLOCKS = 2 * HEADS
+WORDS = CHANNELS // 2
+FLIPS = WORDS // P
+
+FLOPS = 2 * HEIGHT * WIDTH * CHANNELS * OUT_BLOCKS * HEAD_DIM + 2 * WIDTH * HEADS * HEIGHT * HEAD_DIM * HEAD_DIM
+
+
+def tile_linear_retention_pa_t_kernel(tc, x, Wk, bk, Wv, bv, out):
+    nc = tc.nc
+
+    x_slabs = x.rearrange("b (g p t) w e -> (b g) w p t e", g=HEIGHT_PASSES, p=P, t=PACK)
+    out_columns = out.rearrange("b w n d e -> (b w) d n e")
+
+    with ExitStack() as ctx:
+        ctx.enter_context(tc.manual_schedule())
+        const = ctx.enter_context(tc.tile_pool(name="const", bufs=1))
+        rows_pool = ctx.enter_context(tc.tile_pool(name="rows", bufs=SLABS))
+        grouped_pool = ctx.enter_context(tc.tile_pool(name="grouped", bufs=3))
+        x_mx_pool = ctx.enter_context(tc.tile_pool(name="x_mx", bufs=3))
+        kv_pool = ctx.enter_context(tc.tile_pool(name="kv", bufs=2))
+        flip_psum = ctx.enter_context(tc.psum_pool(name="flip_psum", bufs=4))
+        proj_psum = ctx.enter_context(tc.psum_pool(name="proj_psum", bufs=OUT_BLOCKS))
+
+        ident = const.tile([P, P], F32)
+        make_identity(nc, ident[:])
+
+        bias = const.tile([P, OUT_BLOCKS, HEAD_DIM], BF16)
+        nc.scalar.dma_start(
+            out=bias[:, 0:HEADS, :].rearrange("p o n -> p (o n)"), in_=bk.partition_broadcast(P)
+        )
+        nc.scalar.dma_start(
+            out=bias[:, HEADS:OUT_BLOCKS, :].rearrange("p o n -> p (o n)"), in_=bv.partition_broadcast(P)
+        )
+
+        w_rows = const.tile([P, ROW_TILES, CHANNELS], BF16)
+        nc.sync.dma_start(out=w_rows[:, 0:HEADS, :], in_=Wk.rearrange("(o p) e -> p o e", p=P))
+        nc.sync.dma_start(out=w_rows[:, HEADS:OUT_BLOCKS, :], in_=Wv.rearrange("(o p) e -> p o e", p=P))
+        x_rows = []
+        for i in range(SLABS):
+            w, g = divmod(i, HEIGHT_PASSES)
+            rows = rows_pool.tile([P, ROW_TILES, CHANNELS], BF16)
+            nc.sync.dma_start(out=rows[:], in_=x_slabs[g, w])
+            x_rows.append(rows)
+
+        out_sb = const.tile([P, WIDTH, HEADS, HEAD_DIM], F32)
+
+        def transpose_slab(rows):
+            banks = []
+            for r in range(ROW_TILES):
+                words = rows[:, r, :].bitcast(F32)
+                bank = flip_psum.tile([P, FLIPS, P], F32, tag="flip")
+                for s in range(FLIPS):
+                    nc.tensor.transpose(bank[:, s, :], words[:, s * P : (s + 1) * P], ident[:])
+                banks.append(bank)
+            return banks
+
+        def group_slab(copy, banks):
+            grouped = grouped_pool.tile([P, ROW_TILES * CHANNELS], BF16, align_bytes=64)
+            pairs = grouped[:].bitcast(F32).rearrange(
+                "p (r c m u) -> p r c m u", r=ROW_TILES, c=CHANNEL_PASSES, m=P, u=2
+            )
+            for r in range(ROW_TILES):
+                copy(out=pairs[:, r], in_=banks[r][:].rearrange("p (c u) m -> p c m u", u=2))
+            return grouped
+
+        def quantise_slab(pool, grouped):
+            codes = pool.tile([P, ROW_TILES, CHANNEL_PASSES, P], U32, tag="codes", align_bytes=64)
+            scales = pool.tile([P, ROW_TILES, CHANNEL_PASSES, P], U8, tag="scales", align_bytes=64)
+            nc.vector.quantize_mx(
+                out=codes[:].rearrange("p r c m -> p (r c m)").bitcast(FP8X4),
+                scales=scales[:].rearrange("p r c m -> p (r c m)"),
+                in_=grouped[:],
+            )
+            return codes, scales
+
+        def project_slab(x_codes, x_scales):
+            accs = []
+            for o in range(OUT_BLOCKS):
+                acc = proj_psum.tile([P, PACK, HEAD_DIM], F32, tag="proj")
+                for t in range(PACK):
+                    for c in range(CHANNEL_PASSES):
+                        nc.tensor.matmul_mx(
+                            out=acc[:, t, :],
+                            lhsT=x_codes[:, t, c, :].bitcast(FP8X4),
+                            lhsT_scale=x_scales[:, t, c, :],
+                            rhs=w_codes[:, o, c, :].bitcast(FP8X4),
+                            rhs_scale=w_scales[:, o, c, :],
+                            start=(c == 0),
+                            stop=(c == CHANNEL_PASSES - 1),
+                        )
+                accs.append(acc)
+            return accs
+
+        def add_bias(kv_grouped, accs, o):
+            nc.vector.tensor_tensor(
+                out=kv_grouped[:, o],
+                in0=accs[o][:].rearrange("p t n -> p n t"),
+                in1=bias[:, o, :].unsqueeze(2).to_broadcast([P, HEAD_DIM, PACK]),
+                op=mybir.AluOpType.add,
+            )
+
+        def relu_k(kv_grouped):
+            nc.scalar.activation(
+                out=kv_grouped[:, 0:HEADS],
+                in_=kv_grouped[:, 0:HEADS],
+                func=mybir.ActivationFunctionType.Relu,
+            )
+
+        def quantise_kv(kv_codes, kv_scales, g, kv_grouped):
+            nc.vector.quantize_mx(
+                out=kv_codes[:, g].rearrange("p o n -> p (o n)").bitcast(FP8X4),
+                scales=kv_scales[:, g].rearrange("p o n -> p (o n)"),
+                in_=kv_grouped[:].rearrange("p o n t -> p (o n t)"),
+            )
+
+        def state_of_column(w, kv_codes, kv_scales):
+            state = flip_psum.tile([P, FLIPS, P], F32, tag="flip")
+            for n in range(HEADS):
+                for g in range(HEIGHT_PASSES):
+                    nc.tensor.matmul_mx(
+                        out=state[:, n, :],
+                        lhsT=kv_codes[:, g, n, :].bitcast(FP8X4),
+                        lhsT_scale=kv_scales[:, g, n, :],
+                        rhs=kv_codes[:, g, HEADS + n, :].bitcast(FP8X4),
+                        rhs_scale=kv_scales[:, g, HEADS + n, :],
+                        start=(g == 0),
+                        stop=(g == HEIGHT_PASSES - 1),
+                    )
+            nc.scalar.copy(out=out_sb[:, w], in_=state[:, 0:HEADS, :])
+            nc.sync.dma_start(out=out_columns[w], in_=out_sb[:, w])
+
+        w_grouped = group_slab(nc.vector.tensor_copy, transpose_slab(w_rows))
+        x_grouped = {}
+        for i in range(2):
+            x_grouped[i] = group_slab(nc.scalar.copy, transpose_slab(x_rows[i]))
+        w_codes, w_scales = quantise_slab(const, w_grouped)
+        x_mx = {0: quantise_slab(x_mx_pool, x_grouped[0])}
+
+        kv_grouped = {}
+        kv_mx = {}
+
+        def quantise_kv_of_slab(i):
+            w, g = divmod(i, HEIGHT_PASSES)
+            if g == 0:
+                kv_codes = kv_pool.tile([P, HEIGHT_PASSES, OUT_BLOCKS, HEAD_DIM], U32, align_bytes=64)
+                kv_scales = kv_pool.tile([P, HEIGHT_PASSES, OUT_BLOCKS, HEAD_DIM], U8, align_bytes=64)
+                kv_mx[w] = (kv_codes, kv_scales)
+            quantise_kv(kv_mx[w][0], kv_mx[w][1], g, kv_grouped[i])
+
+        for i in range(SLABS):
+            accs = project_slab(x_mx[i][0], x_mx[i][1])
+            kv_tile = kv_pool.tile([P, OUT_BLOCKS, HEAD_DIM, PACK], BF16, align_bytes=64)
+            kv_grouped[i] = kv_tile
+            add_bias(kv_tile, accs, 0)
+            if i >= 1:
+                quantise_kv_of_slab(i - 1)
+            add_bias(kv_tile, accs, 1)
+            relu_k(kv_tile)
+            if i + 1 < SLABS:
+                x_mx[i + 1] = quantise_slab(x_mx_pool, x_grouped[i + 1])
+            add_bias(kv_tile, accs, 2)
+            add_bias(kv_tile, accs, 3)
+            if i >= HEIGHT_PASSES and i % HEIGHT_PASSES == 0:
+                w = i // HEIGHT_PASSES - 1
+                state_of_column(w, kv_mx[w][0], kv_mx[w][1])
+            if i + 2 < SLABS:
+                x_grouped[i + 2] = group_slab(nc.scalar.copy, transpose_slab(x_rows[i + 2]))
+
+        quantise_kv_of_slab(SLABS - 1)
+        state_of_column(WIDTH - 1, kv_mx[WIDTH - 1][0], kv_mx[WIDTH - 1][1])

@@ -26,6 +26,7 @@ SLABS = WIDTH * HEIGHT_PASSES
 OUT_BLOCKS = 2 * HEADS
 WORDS = CHANNELS // 2
 FLIPS = WORDS // P
+LEAD = 3
 
 FLOPS = 2 * HEIGHT * WIDTH * CHANNELS * OUT_BLOCKS * HEAD_DIM + 2 * WIDTH * HEADS * HEIGHT * HEAD_DIM * HEAD_DIM
 
@@ -39,10 +40,10 @@ def tile_linear_retention_pa_t_kernel(tc, x, Wk, bk, Wv, bv, out):
     with ExitStack() as ctx:
         ctx.enter_context(tc.manual_schedule())
         const = ctx.enter_context(tc.tile_pool(name="const", bufs=1))
-        rows_pool = ctx.enter_context(tc.tile_pool(name="rows", bufs=SLABS))
+        rows_pool = ctx.enter_context(tc.tile_pool(name="rows", bufs=SLABS * ROW_TILES))
         grouped_pool = ctx.enter_context(tc.tile_pool(name="grouped", bufs=3))
         x_mx_pool = ctx.enter_context(tc.tile_pool(name="x_mx", bufs=3))
-        kv_pool = ctx.enter_context(tc.tile_pool(name="kv", bufs=2))
+        kv_pool = ctx.enter_context(tc.tile_pool(name="kv", bufs=3))
         flip_psum = ctx.enter_context(tc.psum_pool(name="flip_psum", bufs=4))
         proj_psum = ctx.enter_context(tc.psum_pool(name="proj_psum", bufs=OUT_BLOCKS))
 
@@ -57,22 +58,28 @@ def tile_linear_retention_pa_t_kernel(tc, x, Wk, bk, Wv, bv, out):
             out=bias[:, HEADS:OUT_BLOCKS, :].rearrange("p o n -> p (o n)"), in_=bv.partition_broadcast(P)
         )
 
-        w_rows = const.tile([P, ROW_TILES, CHANNELS], BF16)
-        nc.sync.dma_start(out=w_rows[:, 0:HEADS, :], in_=Wk.rearrange("(o p) e -> p o e", p=P))
-        nc.sync.dma_start(out=w_rows[:, HEADS:OUT_BLOCKS, :], in_=Wv.rearrange("(o p) e -> p o e", p=P))
+        w_rows = []
+        for weights in (Wk, Wv):
+            for n in range(HEADS):
+                rows = const.tile([P, CHANNELS], BF16, name="w_rows%d" % len(w_rows))
+                nc.sync.dma_start(out=rows[:], in_=weights[n * HEAD_DIM : (n + 1) * HEAD_DIM, :])
+                w_rows.append(rows)
         x_rows = []
         for i in range(SLABS):
             w, g = divmod(i, HEIGHT_PASSES)
-            rows = rows_pool.tile([P, ROW_TILES, CHANNELS], BF16)
-            nc.sync.dma_start(out=rows[:], in_=x_slabs[g, w])
-            x_rows.append(rows)
+            slab_rows = []
+            for t in range(ROW_TILES):
+                rows = rows_pool.tile([P, CHANNELS], BF16)
+                nc.sync.dma_start(out=rows[:], in_=x_slabs[g, w][:, t, :])
+                slab_rows.append(rows)
+            x_rows.append(slab_rows)
 
         out_sb = const.tile([P, WIDTH, HEADS, HEAD_DIM], F32)
 
-        def transpose_slab(rows):
+        def transpose_slab(slab_rows):
             banks = []
             for r in range(ROW_TILES):
-                words = rows[:, r, :].bitcast(F32)
+                words = slab_rows[r][:].bitcast(F32)
                 bank = flip_psum.tile([P, FLIPS, P], F32, tag="flip")
                 for s in range(FLIPS):
                     nc.tensor.transpose(bank[:, s, :], words[:, s * P : (s + 1) * P], ident[:])
@@ -154,13 +161,8 @@ def tile_linear_retention_pa_t_kernel(tc, x, Wk, bk, Wv, bv, out):
             nc.scalar.copy(out=out_sb[:, w], in_=state[:, 0:HEADS, :])
             nc.sync.dma_start(out=out_columns[w], in_=out_sb[:, w])
 
-        w_grouped = group_slab(nc.vector.tensor_copy, transpose_slab(w_rows))
         x_grouped = {}
-        for i in range(2):
-            x_grouped[i] = group_slab(nc.scalar.copy, transpose_slab(x_rows[i]))
-        w_codes, w_scales = quantise_slab(const, w_grouped)
-        x_mx = {0: quantise_slab(x_mx_pool, x_grouped[0])}
-
+        x_mx = {}
         kv_grouped = {}
         kv_mx = {}
 
@@ -172,24 +174,36 @@ def tile_linear_retention_pa_t_kernel(tc, x, Wk, bk, Wv, bv, out):
                 kv_mx[w] = (kv_codes, kv_scales)
             quantise_kv(kv_mx[w][0], kv_mx[w][1], g, kv_grouped[i])
 
+        w_grouped = group_slab(nc.vector.tensor_copy, transpose_slab(w_rows))
+        grouped_slabs = 2
+        for j in range(grouped_slabs):
+            x_grouped[j] = group_slab(nc.scalar.copy, transpose_slab(x_rows[j]))
+        w_codes, w_scales = quantise_slab(const, w_grouped)
+        for j in range(grouped_slabs):
+            x_mx[j] = quantise_slab(x_mx_pool, x_grouped[j])
+        quantised_slabs = grouped_slabs
+
         for i in range(SLABS):
             accs = project_slab(x_mx[i][0], x_mx[i][1])
+            if i > HEIGHT_PASSES and (i - 1) % HEIGHT_PASSES == 0:
+                w = (i - 1) // HEIGHT_PASSES - 1
+                state_of_column(w, kv_mx[w][0], kv_mx[w][1])
+
             kv_tile = kv_pool.tile([P, OUT_BLOCKS, HEAD_DIM, PACK], BF16, align_bytes=64)
             kv_grouped[i] = kv_tile
-            add_bias(kv_tile, accs, 0)
+            for o in range(OUT_BLOCKS):
+                add_bias(kv_tile, accs, o)
+            for j in range(quantised_slabs, grouped_slabs):
+                x_mx[j] = quantise_slab(x_mx_pool, x_grouped[j])
+            quantised_slabs = grouped_slabs
             if i >= 1:
                 quantise_kv_of_slab(i - 1)
-            add_bias(kv_tile, accs, 1)
+
+            for j in range(grouped_slabs, min(i + LEAD + 1, SLABS)):
+                x_grouped[j] = group_slab(nc.scalar.copy, transpose_slab(x_rows[j]))
+            grouped_slabs = max(grouped_slabs, min(i + LEAD + 1, SLABS))
+
             relu_k(kv_tile)
-            if i + 1 < SLABS:
-                x_mx[i + 1] = quantise_slab(x_mx_pool, x_grouped[i + 1])
-            add_bias(kv_tile, accs, 2)
-            add_bias(kv_tile, accs, 3)
-            if i >= HEIGHT_PASSES and i % HEIGHT_PASSES == 0:
-                w = i // HEIGHT_PASSES - 1
-                state_of_column(w, kv_mx[w][0], kv_mx[w][1])
-            if i + 2 < SLABS:
-                x_grouped[i + 2] = group_slab(nc.scalar.copy, transpose_slab(x_rows[i + 2]))
 
         quantise_kv_of_slab(SLABS - 1)
         state_of_column(WIDTH - 1, kv_mx[WIDTH - 1][0], kv_mx[WIDTH - 1][1])

@@ -26,7 +26,7 @@ SLABS = WIDTH * HEIGHT_PASSES
 OUT_BLOCKS = 2 * HEADS
 WORDS = CHANNELS // 2
 FLIPS = WORDS // P
-LEAD = 3
+LEAD = 2
 
 FLOPS = 2 * HEIGHT * WIDTH * CHANNELS * OUT_BLOCKS * HEAD_DIM + 2 * WIDTH * HEADS * HEIGHT * HEAD_DIM * HEAD_DIM
 
@@ -175,13 +175,10 @@ def tile_linear_retention_pa_t_kernel(tc, x, Wk, bk, Wv, bv, out):
             quantise_kv(kv_mx[w][0], kv_mx[w][1], g, kv_grouped[i])
 
         w_grouped = group_slab(nc.vector.tensor_copy, transpose_slab(w_rows))
-        grouped_slabs = 2
-        for j in range(grouped_slabs):
+        for j in range(LEAD):
             x_grouped[j] = group_slab(nc.scalar.copy, transpose_slab(x_rows[j]))
         w_codes, w_scales = quantise_slab(const, w_grouped)
-        for j in range(grouped_slabs):
-            x_mx[j] = quantise_slab(x_mx_pool, x_grouped[j])
-        quantised_slabs = grouped_slabs
+        x_mx[0] = quantise_slab(x_mx_pool, x_grouped[0])
 
         for i in range(SLABS):
             accs = project_slab(x_mx[i][0], x_mx[i][1])
@@ -191,17 +188,16 @@ def tile_linear_retention_pa_t_kernel(tc, x, Wk, bk, Wv, bv, out):
 
             kv_tile = kv_pool.tile([P, OUT_BLOCKS, HEAD_DIM, PACK], BF16, align_bytes=64)
             kv_grouped[i] = kv_tile
-            for o in range(OUT_BLOCKS):
+            add_bias(kv_tile, accs, 0)
+            if i + 1 < SLABS:
+                x_mx[i + 1] = quantise_slab(x_mx_pool, x_grouped[i + 1])
+            for o in range(1, OUT_BLOCKS):
                 add_bias(kv_tile, accs, o)
-            for j in range(quantised_slabs, grouped_slabs):
-                x_mx[j] = quantise_slab(x_mx_pool, x_grouped[j])
-            quantised_slabs = grouped_slabs
             if i >= 1:
                 quantise_kv_of_slab(i - 1)
 
-            for j in range(grouped_slabs, min(i + LEAD + 1, SLABS)):
-                x_grouped[j] = group_slab(nc.scalar.copy, transpose_slab(x_rows[j]))
-            grouped_slabs = max(grouped_slabs, min(i + LEAD + 1, SLABS))
+            if i + LEAD < SLABS:
+                x_grouped[i + LEAD] = group_slab(nc.scalar.copy, transpose_slab(x_rows[i + LEAD]))
 
             relu_k(kv_tile)
 

@@ -38,7 +38,6 @@ def tile_linear_retention_pa_t_kernel(tc, x, Wk, bk, Wv, bv, out):
     out_columns = out.rearrange("b w n d e -> (b w) d n e")
 
     with ExitStack() as ctx:
-        ctx.enter_context(tc.manual_schedule())
         const = ctx.enter_context(tc.tile_pool(name="const", bufs=1))
         rows_pool = ctx.enter_context(tc.tile_pool(name="rows", bufs=SLABS * ROW_TILES))
         grouped_pool = ctx.enter_context(tc.tile_pool(name="grouped", bufs=3))

@@ -12,6 +12,7 @@ FP8X4 = mybir.dt.float8_e4m3fn_x4
 P = 128
 PACK = 4
 K_PASS = P * PACK
+MX_ALIGN = 64
 
 HEIGHT = 1024
 WIDTH = 8
@@ -24,9 +25,12 @@ CHANNEL_PASSES = CHANNELS // K_PASS
 HEIGHT_PASSES = HEIGHT // K_PASS
 SLABS = WIDTH * HEIGHT_PASSES
 OUT_BLOCKS = 2 * HEADS
-WORDS = CHANNELS // 2
+PAIR = 2
+WORDS = CHANNELS // PAIR
 FLIPS = WORDS // P
 LEAD = 2
+FLIP_BANKS = ROW_TILES
+SPARE = 1
 
 FLOPS = 2 * HEIGHT * WIDTH * CHANNELS * OUT_BLOCKS * HEAD_DIM + 2 * WIDTH * HEADS * HEIGHT * HEAD_DIM * HEAD_DIM
 
@@ -34,28 +38,29 @@ FLOPS = 2 * HEIGHT * WIDTH * CHANNELS * OUT_BLOCKS * HEAD_DIM + 2 * WIDTH * HEAD
 def tile_linear_retention_pa_t_kernel(tc, x, Wk, bk, Wv, bv, out):
     nc = tc.nc
 
-    x_slabs = x.rearrange("b (g p t) w e -> (b g) w p t e", g=HEIGHT_PASSES, p=P, t=PACK)
+    x_slabs = x.rearrange("b (g p t) w a -> (b g) w p t a", g=HEIGHT_PASSES, p=P, t=PACK)
     out_columns = out.rearrange("b w n d e -> (b w) d n e")
 
     with ExitStack() as ctx:
+        ctx.enter_context(tc.manual_schedule())
         const = ctx.enter_context(tc.tile_pool(name="const", bufs=1))
         rows_pool = ctx.enter_context(tc.tile_pool(name="rows", bufs=SLABS * ROW_TILES))
-        grouped_pool = ctx.enter_context(tc.tile_pool(name="grouped", bufs=3))
-        x_mx_pool = ctx.enter_context(tc.tile_pool(name="x_mx", bufs=3))
-        kv_pool = ctx.enter_context(tc.tile_pool(name="kv", bufs=3))
-        flip_psum = ctx.enter_context(tc.psum_pool(name="flip_psum", bufs=4))
+        grouped_pool = ctx.enter_context(tc.tile_pool(name="grouped", bufs=LEAD + 1))
+        x_mx_pool = ctx.enter_context(tc.tile_pool(name="x_mx", bufs=2 + SPARE))
+        kv_pool = ctx.enter_context(tc.tile_pool(name="kv", bufs=2 + SPARE))
+        flip_psum = ctx.enter_context(tc.psum_pool(name="flip_psum", bufs=FLIP_BANKS))
         proj_psum = ctx.enter_context(tc.psum_pool(name="proj_psum", bufs=OUT_BLOCKS))
 
         ident = const.tile([P, P], F32)
         make_identity(nc, ident[:])
 
+        ones = const.tile([P, P], BF16)
+        nc.vector.memset(ones[:], 1.0)
+        bias_row = const.tile([P, OUT_BLOCKS * HEAD_DIM], BF16)
+        nc.vector.memset(bias_row[:], 0.0)
+        nc.scalar.dma_start(out=bias_row[0:1, 0 : HEADS * HEAD_DIM], in_=bk.unsqueeze(0))
+        nc.scalar.dma_start(out=bias_row[0:1, HEADS * HEAD_DIM : OUT_BLOCKS * HEAD_DIM], in_=bv.unsqueeze(0))
         bias = const.tile([P, OUT_BLOCKS, HEAD_DIM], BF16)
-        nc.scalar.dma_start(
-            out=bias[:, 0:HEADS, :].rearrange("p o n -> p (o n)"), in_=bk.partition_broadcast(P)
-        )
-        nc.scalar.dma_start(
-            out=bias[:, HEADS:OUT_BLOCKS, :].rearrange("p o n -> p (o n)"), in_=bv.partition_broadcast(P)
-        )
 
         w_rows = []
         for weights in (Wk, Wv):
@@ -80,29 +85,36 @@ def tile_linear_retention_pa_t_kernel(tc, x, Wk, bk, Wv, bv, out):
             for r in range(ROW_TILES):
                 words = slab_rows[r][:].bitcast(F32)
                 bank = flip_psum.tile([P, FLIPS, P], F32, tag="flip")
-                for s in range(FLIPS):
-                    nc.tensor.transpose(bank[:, s, :], words[:, s * P : (s + 1) * P], ident[:])
+                for f in range(FLIPS):
+                    nc.tensor.transpose(bank[:, f, :], words[:, f * P : (f + 1) * P], ident[:])
                 banks.append(bank)
             return banks
 
         def group_slab(copy, banks):
-            grouped = grouped_pool.tile([P, ROW_TILES * CHANNELS], BF16, align_bytes=64)
+            grouped = grouped_pool.tile([P, ROW_TILES * CHANNELS], BF16, align_bytes=MX_ALIGN)
             pairs = grouped[:].bitcast(F32).rearrange(
-                "p (r c m u) -> p r c m u", r=ROW_TILES, c=CHANNEL_PASSES, m=P, u=2
+                "p (r c m u) -> p r c m u", r=ROW_TILES, c=CHANNEL_PASSES, m=P, u=PAIR
             )
             for r in range(ROW_TILES):
-                copy(out=pairs[:, r], in_=banks[r][:].rearrange("p (c u) m -> p c m u", u=2))
+                copy(out=pairs[:, r], in_=banks[r][:].rearrange("p (c u) m -> p c m u", u=PAIR))
             return grouped
 
         def quantise_slab(pool, grouped):
-            codes = pool.tile([P, ROW_TILES, CHANNEL_PASSES, P], U32, tag="codes", align_bytes=64)
-            scales = pool.tile([P, ROW_TILES, CHANNEL_PASSES, P], U8, tag="scales", align_bytes=64)
+            codes = pool.tile([P, ROW_TILES, CHANNEL_PASSES, P], U32, tag="codes", align_bytes=MX_ALIGN)
+            scales = pool.tile([P, ROW_TILES, CHANNEL_PASSES, P], U8, tag="scales", align_bytes=MX_ALIGN)
             nc.vector.quantize_mx(
                 out=codes[:].rearrange("p r c m -> p (r c m)").bitcast(FP8X4),
                 scales=scales[:].rearrange("p r c m -> p (r c m)"),
                 in_=grouped[:],
             )
             return codes, scales
+
+        def spread_bias():
+            spread = flip_psum.tile([P, FLIPS, P], F32, tag="flip")
+            nc.tensor.matmul(
+                out=spread[:].rearrange("p o j -> p (o j)"), lhsT=ones[:], rhs=bias_row[:], start=True, stop=True
+            )
+            nc.vector.tensor_copy(out=bias[:], in_=spread[:])
 
         def project_slab(x_codes, x_scales):
             accs = []
@@ -122,26 +134,26 @@ def tile_linear_retention_pa_t_kernel(tc, x, Wk, bk, Wv, bv, out):
                 accs.append(acc)
             return accs
 
-        def add_bias(kv_grouped, accs, o):
+        def add_bias(kv_tile, accs, o):
             nc.vector.tensor_tensor(
-                out=kv_grouped[:, o],
-                in0=accs[o][:].rearrange("p t n -> p n t"),
+                out=kv_tile[:, o],
+                in0=accs[o][:].rearrange("p t j -> p j t"),
                 in1=bias[:, o, :].unsqueeze(2).to_broadcast([P, HEAD_DIM, PACK]),
                 op=mybir.AluOpType.add,
             )
 
-        def relu_k(kv_grouped):
+        def relu_k(kv_tile):
             nc.scalar.activation(
-                out=kv_grouped[:, 0:HEADS],
-                in_=kv_grouped[:, 0:HEADS],
+                out=kv_tile[:, 0:HEADS],
+                in_=kv_tile[:, 0:HEADS],
                 func=mybir.ActivationFunctionType.Relu,
             )
 
-        def quantise_kv(kv_codes, kv_scales, g, kv_grouped):
+        def quantise_kv(kv_codes, kv_scales, g, kv_tile):
             nc.vector.quantize_mx(
-                out=kv_codes[:, g].rearrange("p o n -> p (o n)").bitcast(FP8X4),
-                scales=kv_scales[:, g].rearrange("p o n -> p (o n)"),
-                in_=kv_grouped[:].rearrange("p o n t -> p (o n t)"),
+                out=kv_codes[:, g].rearrange("p o j -> p (o j)").bitcast(FP8X4),
+                scales=kv_scales[:, g].rearrange("p o j -> p (o j)"),
+                in_=kv_tile[:].rearrange("p o j t -> p (o j t)"),
             )
 
         def state_of_column(w, kv_codes, kv_scales):
@@ -162,22 +174,23 @@ def tile_linear_retention_pa_t_kernel(tc, x, Wk, bk, Wv, bv, out):
 
         x_grouped = {}
         x_mx = {}
-        kv_grouped = {}
+        kv_tiles = {}
         kv_mx = {}
 
         def quantise_kv_of_slab(i):
             w, g = divmod(i, HEIGHT_PASSES)
             if g == 0:
-                kv_codes = kv_pool.tile([P, HEIGHT_PASSES, OUT_BLOCKS, HEAD_DIM], U32, align_bytes=64)
-                kv_scales = kv_pool.tile([P, HEIGHT_PASSES, OUT_BLOCKS, HEAD_DIM], U8, align_bytes=64)
+                kv_codes = kv_pool.tile([P, HEIGHT_PASSES, OUT_BLOCKS, HEAD_DIM], U32, align_bytes=MX_ALIGN)
+                kv_scales = kv_pool.tile([P, HEIGHT_PASSES, OUT_BLOCKS, HEAD_DIM], U8, align_bytes=MX_ALIGN)
                 kv_mx[w] = (kv_codes, kv_scales)
-            quantise_kv(kv_mx[w][0], kv_mx[w][1], g, kv_grouped[i])
+            quantise_kv(kv_mx[w][0], kv_mx[w][1], g, kv_tiles[i])
 
         w_grouped = group_slab(nc.vector.tensor_copy, transpose_slab(w_rows))
         for j in range(LEAD):
             x_grouped[j] = group_slab(nc.scalar.copy, transpose_slab(x_rows[j]))
         w_codes, w_scales = quantise_slab(const, w_grouped)
         x_mx[0] = quantise_slab(x_mx_pool, x_grouped[0])
+        spread_bias()
 
         for i in range(SLABS):
             accs = project_slab(x_mx[i][0], x_mx[i][1])
@@ -185,8 +198,8 @@ def tile_linear_retention_pa_t_kernel(tc, x, Wk, bk, Wv, bv, out):
                 w = (i - 1) // HEIGHT_PASSES - 1
                 state_of_column(w, kv_mx[w][0], kv_mx[w][1])
 
-            kv_tile = kv_pool.tile([P, OUT_BLOCKS, HEAD_DIM, PACK], BF16, align_bytes=64)
-            kv_grouped[i] = kv_tile
+            kv_tile = kv_pool.tile([P, OUT_BLOCKS, HEAD_DIM, PACK], BF16, align_bytes=MX_ALIGN)
+            kv_tiles[i] = kv_tile
             add_bias(kv_tile, accs, 0)
             if i + 1 < SLABS:
                 x_mx[i + 1] = quantise_slab(x_mx_pool, x_grouped[i + 1])

@@ -116,25 +116,44 @@ def tile_linear_retention_pa_t_kernel(tc, x, Wk, bk, Wv, bv, out):
             )
             nc.vector.tensor_copy(out=bias[:], in_=spread[:])
 
+        def w_operand(b, c):
+            if b == 0:
+                lo, width = c * HEADS * P, HEADS * P
+            else:
+                lo, width = ((HEADS + b - 1) * CHANNEL_PASSES + c) * P, P
+            return w_codes[:, lo : lo + width].bitcast(FP8X4), w_scales[:, lo : lo + width]
+
         def project_slab(x_codes, x_scales):
             accs = []
-            for o in range(OUT_BLOCKS):
-                acc = proj_psum.tile([P, PACK, HEAD_DIM], F32, tag="proj")
-                for t in range(PACK):
+            for b, ts in ((0, (0, 1)), (0, (2, 3)), (1, (0, 1, 2, 3)), (2, (0, 1, 2, 3))):
+                acc = proj_psum.tile([P, len(ts), PACK * HEAD_DIM // len(ts)], F32, tag="proj")
+                for at, t in enumerate(ts):
                     for c in range(CHANNEL_PASSES):
+                        rhs, rhs_scale = w_operand(b, c)
                         nc.tensor.matmul_mx(
-                            out=acc[:, t, :],
+                            out=acc[:, at, :],
                             lhsT=x_codes[:, t, c, :].bitcast(FP8X4),
                             lhsT_scale=x_scales[:, t, c, :],
-                            rhs=w_codes[:, o, c, :].bitcast(FP8X4),
-                            rhs_scale=w_scales[:, o, c, :],
+                            rhs=rhs,
+                            rhs_scale=rhs_scale,
                             start=(c == 0),
                             stop=(c == CHANNEL_PASSES - 1),
                         )
                 accs.append(acc)
             return accs
 
-        def add_bias(kv_tile, accs, o):
+        def add_bias(k_pairs, kv_tile, accs, o):
+            if o < HEADS:
+                nc.vector.tensor_tensor(
+                    out=k_pairs[:, o],
+                    in0=accs[o][:].rearrange("p t j -> p j t"),
+                    in1=bias[:, 0:HEADS]
+                    .rearrange("p n j -> p (n j)")
+                    .unsqueeze(2)
+                    .to_broadcast([P, HEADS * HEAD_DIM, PAIR]),
+                    op=mybir.AluOpType.add,
+                )
+                return
             nc.vector.tensor_tensor(
                 out=kv_tile[:, o],
                 in0=accs[o][:].rearrange("p t j -> p j t"),
@@ -142,10 +161,10 @@ def tile_linear_retention_pa_t_kernel(tc, x, Wk, bk, Wv, bv, out):
                 op=mybir.AluOpType.add,
             )
 
-        def relu_k(kv_tile):
+        def relu_k(k_pairs, kv_tile):
             nc.scalar.activation(
-                out=kv_tile[:, 0:HEADS],
-                in_=kv_tile[:, 0:HEADS],
+                out=kv_tile[:, 0:HEADS].rearrange("p n j (a e) -> p (n j) a e", a=PAIR),
+                in_=k_pairs[:].rearrange("p a j e -> p j a e"),
                 func=mybir.ActivationFunctionType.Relu,
             )
 
@@ -185,10 +204,22 @@ def tile_linear_retention_pa_t_kernel(tc, x, Wk, bk, Wv, bv, out):
                 kv_mx[w] = (kv_codes, kv_scales)
             quantise_kv(kv_mx[w][0], kv_mx[w][1], g, kv_tiles[i])
 
-        w_grouped = group_slab(nc.vector.tensor_copy, transpose_slab(w_rows))
+        w_banks = transpose_slab(w_rows)
+        w_grouped = grouped_pool.tile([P, ROW_TILES * CHANNELS], BF16, name="grouped", align_bytes=MX_ALIGN)
+        w_words = w_grouped[:].bitcast(F32)
+        half = ROW_TILES * WORDS // 2
+        k_words = w_words[:, 0:half].rearrange("p (c n m u) -> p n c m u", c=CHANNEL_PASSES, n=HEADS, u=PAIR)
+        v_words = w_words[:, half : 2 * half].rearrange("p (n c m u) -> p n c m u", c=CHANNEL_PASSES, n=HEADS, u=PAIR)
+        for r in range(ROW_TILES):
+            nc.vector.tensor_copy(
+                out=k_words[:, r] if r < HEADS else v_words[:, r - HEADS],
+                in_=w_banks[r][:].rearrange("p (c u) m -> p c m u", u=PAIR),
+            )
         for j in range(LEAD):
             x_grouped[j] = group_slab(nc.scalar.copy, transpose_slab(x_rows[j]))
-        w_codes, w_scales = quantise_slab(const, w_grouped)
+        w_codes_tile, w_scales_tile = quantise_slab(const, w_grouped)
+        w_codes = w_codes_tile[:].rearrange("p r c m -> p (r c m)")
+        w_scales = w_scales_tile[:].rearrange("p r c m -> p (r c m)")
         x_mx[0] = quantise_slab(x_mx_pool, x_grouped[0])
         spread_bias()
 
@@ -200,18 +231,19 @@ def tile_linear_retention_pa_t_kernel(tc, x, Wk, bk, Wv, bv, out):
 
             kv_tile = kv_pool.tile([P, OUT_BLOCKS, HEAD_DIM, PACK], BF16, align_bytes=MX_ALIGN)
             kv_tiles[i] = kv_tile
-            add_bias(kv_tile, accs, 0)
+            k_pairs = kv_pool.tile([P, PAIR, HEADS * HEAD_DIM, PAIR], BF16, align_bytes=MX_ALIGN)
+            add_bias(k_pairs, kv_tile, accs, 0)
             if i + 1 < SLABS:
                 x_mx[i + 1] = quantise_slab(x_mx_pool, x_grouped[i + 1])
             for o in range(1, OUT_BLOCKS):
-                add_bias(kv_tile, accs, o)
+                add_bias(k_pairs, kv_tile, accs, o)
             if i >= 1:
                 quantise_kv_of_slab(i - 1)
 
             if i + LEAD < SLABS:
                 x_grouped[i + LEAD] = group_slab(nc.scalar.copy, transpose_slab(x_rows[i + LEAD]))
 
-            relu_k(kv_tile)
+            relu_k(k_pairs, kv_tile)
 
         quantise_kv_of_slab(SLABS - 1)
         state_of_column(WIDTH - 1, kv_mx[WIDTH - 1][0], kv_mx[WIDTH - 1][1])

@@ -62,52 +62,83 @@ def tile_linear_retention_pa_t_kernel(tc, x, Wk, bk, Wv, bv, out):
         nc.scalar.dma_start(out=bias_row[0:1, HEADS * HEAD_DIM : OUT_BLOCKS * HEAD_DIM], in_=bv.unsqueeze(0))
         bias = const.tile([P, OUT_BLOCKS, HEAD_DIM], BF16)
 
-        w_rows = []
-        for weights in (Wk, Wv):
+        w_rows = {}
+        x_rows = {}
+
+        def load_weights(b, weights):
+            w_rows[b] = []
             for n in range(HEADS):
-                rows = const.tile([P, CHANNELS], BF16, name="w_rows%d" % len(w_rows))
+                rows = const.tile([P, CHANNELS], BF16, name="w_rows%d_%d" % (b, n))
                 nc.sync.dma_start(out=rows[:], in_=weights[n * HEAD_DIM : (n + 1) * HEAD_DIM, :])
-                w_rows.append(rows)
-        x_rows = []
-        for i in range(SLABS):
+                w_rows[b].append(rows)
+
+        def load_slab(i):
             w, g = divmod(i, HEIGHT_PASSES)
-            slab_rows = []
+            x_rows[i] = []
             for t in range(ROW_TILES):
                 rows = rows_pool.tile([P, CHANNELS], BF16)
                 nc.sync.dma_start(out=rows[:], in_=x_slabs[g, w][:, t, :])
-                slab_rows.append(rows)
-            x_rows.append(slab_rows)
+                x_rows[i].append(rows)
+
+        load_weights(0, Wk)
+        load_slab(0)
+        load_weights(1, Wv)
+        for i in range(1, SLABS):
+            load_slab(i)
 
         out_sb = const.tile([P, WIDTH, HEADS, HEAD_DIM], F32)
 
-        def transpose_slab(slab_rows):
-            banks = []
-            for r in range(ROW_TILES):
-                words = slab_rows[r][:].bitcast(F32)
-                bank = flip_psum.tile([P, FLIPS, P], F32, tag="flip")
-                for f in range(FLIPS):
-                    nc.tensor.transpose(bank[:, f, :], words[:, f * P : (f + 1) * P], ident[:])
-                banks.append(bank)
-            return banks
+        w_grouped = grouped_pool.tile([P, ROW_TILES * CHANNELS], BF16, name="grouped", align_bytes=MX_ALIGN)
+        w_words = (
+            w_grouped[:]
+            .bitcast(F32)
+            .rearrange("p (b c n m u) -> p b n c m u", b=PAIR, c=CHANNEL_PASSES, n=HEADS, m=P, u=PAIR)
+        )
+        w_codes = const.tile([P, PAIR, CHANNEL_PASSES, HEADS * P], U32, align_bytes=MX_ALIGN)
+        w_scales = const.tile([P, PAIR, CHANNEL_PASSES, HEADS * P], U8, align_bytes=MX_ALIGN)
+        x_grouped = {}
+        x_codes = {}
+        x_scales = {}
 
-        def group_slab(copy, banks):
-            grouped = grouped_pool.tile([P, ROW_TILES * CHANNELS], BF16, align_bytes=MX_ALIGN)
-            pairs = grouped[:].bitcast(F32).rearrange(
+        def turn(rows, words):
+            bank = flip_psum.tile([P, FLIPS, P], F32, tag="flip")
+            for f in range(FLIPS):
+                nc.tensor.transpose(bank[:, f, :], rows[:].bitcast(F32)[:, f * P : (f + 1) * P], ident[:])
+            nc.scalar.copy(out=words, in_=bank[:].rearrange("p (c u) m -> p c m u", u=PAIR))
+
+        def turn_weights(b):
+            for n in range(HEADS):
+                turn(w_rows[b][n], w_words[:, b, n])
+
+        def turn_x(i, ts):
+            if i not in x_grouped:
+                grouped = grouped_pool.tile([P, ROW_TILES * CHANNELS], BF16, name="grouped", align_bytes=MX_ALIGN)
+                x_grouped[i] = grouped
+            words = x_grouped[i][:].bitcast(F32).rearrange(
                 "p (r c m u) -> p r c m u", r=ROW_TILES, c=CHANNEL_PASSES, m=P, u=PAIR
             )
-            for r in range(ROW_TILES):
-                copy(out=pairs[:, r], in_=banks[r][:].rearrange("p (c u) m -> p c m u", u=PAIR))
-            return grouped
+            for t in ts:
+                turn(x_rows[i][t], words[:, t])
 
-        def quantise_slab(pool, grouped):
-            codes = pool.tile([P, ROW_TILES, CHANNEL_PASSES, P], U32, tag="codes", align_bytes=MX_ALIGN)
-            scales = pool.tile([P, ROW_TILES, CHANNEL_PASSES, P], U8, tag="scales", align_bytes=MX_ALIGN)
+        def quantise_weights(b):
+            half = w_grouped[:].rearrange("p (b e) -> p b e", b=PAIR)
             nc.vector.quantize_mx(
-                out=codes[:].rearrange("p r c m -> p (r c m)").bitcast(FP8X4),
-                scales=scales[:].rearrange("p r c m -> p (r c m)"),
-                in_=grouped[:],
+                out=w_codes[:, b].rearrange("p c j -> p (c j)").bitcast(FP8X4),
+                scales=w_scales[:, b].rearrange("p c j -> p (c j)"),
+                in_=half[:, b],
             )
-            return codes, scales
+
+        def quantise_x(i, t0, count):
+            if i not in x_codes:
+                codes = x_mx_pool.tile([P, ROW_TILES, CHANNEL_PASSES, P], U32, align_bytes=MX_ALIGN)
+                scales = x_mx_pool.tile([P, ROW_TILES, CHANNEL_PASSES, P], U8, align_bytes=MX_ALIGN)
+                x_codes[i] = codes
+                x_scales[i] = scales
+            nc.vector.quantize_mx(
+                out=x_codes[i][:, t0 : t0 + count].rearrange("p r c m -> p (r c m)").bitcast(FP8X4),
+                scales=x_scales[i][:, t0 : t0 + count].rearrange("p r c m -> p (r c m)"),
+                in_=x_grouped[i][:, t0 * CHANNELS : (t0 + count) * CHANNELS],
+            )
 
         def spread_bias():
             spread = flip_psum.tile([P, FLIPS, P], F32, tag="flip")
@@ -116,66 +147,73 @@ def tile_linear_retention_pa_t_kernel(tc, x, Wk, bk, Wv, bv, out):
             )
             nc.vector.tensor_copy(out=bias[:], in_=spread[:])
 
-        def w_operand(b, c):
-            if b == 0:
-                lo, width = c * HEADS * P, HEADS * P
+        accs = {}
+        k_pairs = {}
+        kv_tiles = {}
+        kv_mx = {}
+
+        def project(i, a):
+            is_k = a < HEADS
+            ts = (PAIR * a, PAIR * a + 1) if is_k else tuple(range(PACK))
+            width = HEADS * HEAD_DIM if is_k else HEAD_DIM
+            lo = 0 if is_k else (a - HEADS) * HEAD_DIM
+            b = 0 if is_k else 1
+            acc = proj_psum.tile([P, len(ts), width], F32, tag="proj")
+            for at, t in enumerate(ts):
+                for c in range(CHANNEL_PASSES):
+                    nc.tensor.matmul_mx(
+                        out=acc[:, at, :],
+                        lhsT=x_codes[i][:, t, c, :].bitcast(FP8X4),
+                        lhsT_scale=x_scales[i][:, t, c, :],
+                        rhs=w_codes[:, b, c, lo : lo + width].bitcast(FP8X4),
+                        rhs_scale=w_scales[:, b, c, lo : lo + width],
+                        start=(c == 0),
+                        stop=(c == CHANNEL_PASSES - 1),
+                    )
+            accs[i, a] = acc
+
+        def add_bias(i, a):
+            if a == 0:
+                pairs = kv_pool.tile([P, PAIR, HEADS * HEAD_DIM, PAIR], BF16, align_bytes=MX_ALIGN)
+                kv_tile = kv_pool.tile([P, OUT_BLOCKS, HEAD_DIM, PACK], BF16, align_bytes=MX_ALIGN)
+                k_pairs[i] = pairs
+                kv_tiles[i] = kv_tile
+            if a < HEADS:
+                dest = k_pairs[i][:, a]
+                channels = bias[:, 0:HEADS].rearrange("p n j -> p (n j)")
             else:
-                lo, width = ((HEADS + b - 1) * CHANNEL_PASSES + c) * P, P
-            return w_codes[:, lo : lo + width].bitcast(FP8X4), w_scales[:, lo : lo + width]
-
-        def project_slab(x_codes, x_scales):
-            accs = []
-            for b, ts in ((0, (0, 1)), (0, (2, 3)), (1, (0, 1, 2, 3)), (2, (0, 1, 2, 3))):
-                acc = proj_psum.tile([P, len(ts), PACK * HEAD_DIM // len(ts)], F32, tag="proj")
-                for at, t in enumerate(ts):
-                    for c in range(CHANNEL_PASSES):
-                        rhs, rhs_scale = w_operand(b, c)
-                        nc.tensor.matmul_mx(
-                            out=acc[:, at, :],
-                            lhsT=x_codes[:, t, c, :].bitcast(FP8X4),
-                            lhsT_scale=x_scales[:, t, c, :],
-                            rhs=rhs,
-                            rhs_scale=rhs_scale,
-                            start=(c == 0),
-                            stop=(c == CHANNEL_PASSES - 1),
-                        )
-                accs.append(acc)
-            return accs
-
-        def add_bias(k_pairs, kv_tile, accs, o):
-            if o < HEADS:
-                nc.vector.tensor_tensor(
-                    out=k_pairs[:, o],
-                    in0=accs[o][:].rearrange("p t j -> p j t"),
-                    in1=bias[:, 0:HEADS]
-                    .rearrange("p n j -> p (n j)")
-                    .unsqueeze(2)
-                    .to_broadcast([P, HEADS * HEAD_DIM, PAIR]),
-                    op=mybir.AluOpType.add,
-                )
-                return
+                dest = kv_tiles[i][:, a]
+                channels = bias[:, a]
+            heights = PAIR if a < HEADS else PACK
+            width = HEADS * HEAD_DIM if a < HEADS else HEAD_DIM
             nc.vector.tensor_tensor(
-                out=kv_tile[:, o],
-                in0=accs[o][:].rearrange("p t j -> p j t"),
-                in1=bias[:, o, :].unsqueeze(2).to_broadcast([P, HEAD_DIM, PACK]),
+                out=dest,
+                in0=accs[i, a][:].rearrange("p t j -> p j t"),
+                in1=channels.unsqueeze(2).to_broadcast([P, width, heights]),
                 op=mybir.AluOpType.add,
             )
 
-        def relu_k(k_pairs, kv_tile):
+        def relu_k(i):
             nc.scalar.activation(
-                out=kv_tile[:, 0:HEADS].rearrange("p n j (a e) -> p (n j) a e", a=PAIR),
-                in_=k_pairs[:].rearrange("p a j e -> p j a e"),
+                out=kv_tiles[i][:, 0:HEADS].rearrange("p n j (a e) -> p (n j) a e", a=PAIR),
+                in_=k_pairs[i][:].rearrange("p a j e -> p j a e"),
                 func=mybir.ActivationFunctionType.Relu,
             )
 
-        def quantise_kv(kv_codes, kv_scales, g, kv_tile):
+        def quantise_kv(i, o0, count):
+            w, g = divmod(i, HEIGHT_PASSES)
+            if w not in kv_mx:
+                kv_codes = kv_pool.tile([P, HEIGHT_PASSES, OUT_BLOCKS, HEAD_DIM], U32, align_bytes=MX_ALIGN)
+                kv_scales = kv_pool.tile([P, HEIGHT_PASSES, OUT_BLOCKS, HEAD_DIM], U8, align_bytes=MX_ALIGN)
+                kv_mx[w] = (kv_codes, kv_scales)
             nc.vector.quantize_mx(
-                out=kv_codes[:, g].rearrange("p o j -> p (o j)").bitcast(FP8X4),
-                scales=kv_scales[:, g].rearrange("p o j -> p (o j)"),
-                in_=kv_tile[:].rearrange("p o j t -> p (o j t)"),
+                out=kv_mx[w][0][:, g, o0 : o0 + count].rearrange("p o j -> p (o j)").bitcast(FP8X4),
+                scales=kv_mx[w][1][:, g, o0 : o0 + count].rearrange("p o j -> p (o j)"),
+                in_=kv_tiles[i][:, o0 : o0 + count].rearrange("p o j t -> p (o j t)"),
             )
 
-        def state_of_column(w, kv_codes, kv_scales):
+        def state_of_column(w):
+            kv_codes, kv_scales = kv_mx[w]
             state = flip_psum.tile([P, FLIPS, P], F32, tag="flip")
             for n in range(HEADS):
                 for g in range(HEIGHT_PASSES):
@@ -191,59 +229,67 @@ def tile_linear_retention_pa_t_kernel(tc, x, Wk, bk, Wv, bv, out):
             nc.scalar.copy(out=out_sb[:, w], in_=state[:, 0:HEADS, :])
             nc.sync.dma_start(out=out_columns[w], in_=out_sb[:, w])
 
-        x_grouped = {}
-        x_mx = {}
-        kv_tiles = {}
-        kv_mx = {}
+        ALL = tuple(range(ROW_TILES))
 
-        def quantise_kv_of_slab(i):
-            w, g = divmod(i, HEIGHT_PASSES)
-            if g == 0:
-                kv_codes = kv_pool.tile([P, HEIGHT_PASSES, OUT_BLOCKS, HEAD_DIM], U32, align_bytes=MX_ALIGN)
-                kv_scales = kv_pool.tile([P, HEIGHT_PASSES, OUT_BLOCKS, HEAD_DIM], U8, align_bytes=MX_ALIGN)
-                kv_mx[w] = (kv_codes, kv_scales)
-            quantise_kv(kv_mx[w][0], kv_mx[w][1], g, kv_tiles[i])
-
-        w_banks = transpose_slab(w_rows)
-        w_grouped = grouped_pool.tile([P, ROW_TILES * CHANNELS], BF16, name="grouped", align_bytes=MX_ALIGN)
-        w_words = w_grouped[:].bitcast(F32)
-        half = ROW_TILES * WORDS // 2
-        k_words = w_words[:, 0:half].rearrange("p (c n m u) -> p n c m u", c=CHANNEL_PASSES, n=HEADS, u=PAIR)
-        v_words = w_words[:, half : 2 * half].rearrange("p (n c m u) -> p n c m u", c=CHANNEL_PASSES, n=HEADS, u=PAIR)
-        for r in range(ROW_TILES):
-            nc.vector.tensor_copy(
-                out=k_words[:, r] if r < HEADS else v_words[:, r - HEADS],
-                in_=w_banks[r][:].rearrange("p (c u) m -> p c m u", u=PAIR),
-            )
-        for j in range(LEAD):
-            x_grouped[j] = group_slab(nc.scalar.copy, transpose_slab(x_rows[j]))
-        w_codes_tile, w_scales_tile = quantise_slab(const, w_grouped)
-        w_codes = w_codes_tile[:].rearrange("p r c m -> p (r c m)")
-        w_scales = w_scales_tile[:].rearrange("p r c m -> p (r c m)")
-        x_mx[0] = quantise_slab(x_mx_pool, x_grouped[0])
+        turn_weights(0)
         spread_bias()
+        quantise_weights(0)
+        turn_x(0, ALL)
+        quantise_x(0, 0, 2)
+        project(0, 0)
+        turn_weights(1)
+        quantise_x(0, 2, 2)
+        project(0, 1)
+        add_bias(0, 0)
+        quantise_weights(1)
+        turn_x(1, ALL)
+        add_bias(0, 1)
+        project(0, 2)
+        project(0, 3)
+        quantise_x(1, 0, 2)
+        add_bias(0, 2)
+        quantise_x(1, 2, 2)
+        add_bias(0, 3)
+        project(1, 0)
+        turn_x(2, ALL)
+        relu_k(0)
+        project(1, 1)
+        add_bias(1, 0)
+        quantise_x(2, 0, 2)
+        add_bias(1, 1)
+        quantise_x(2, 2, 2)
+        project(1, 2)
+        project(1, 3)
+        add_bias(1, 2)
+        add_bias(1, 3)
+        quantise_kv(0, 0, OUT_BLOCKS)
+        turn_x(3, ALL)
+        relu_k(1)
 
-        for i in range(SLABS):
-            accs = project_slab(x_mx[i][0], x_mx[i][1])
+        for i in range(2, SLABS - 1):
+            for a in range(OUT_BLOCKS):
+                project(i, a)
             if i > HEIGHT_PASSES and (i - 1) % HEIGHT_PASSES == 0:
-                w = (i - 1) // HEIGHT_PASSES - 1
-                state_of_column(w, kv_mx[w][0], kv_mx[w][1])
-
-            kv_tile = kv_pool.tile([P, OUT_BLOCKS, HEAD_DIM, PACK], BF16, align_bytes=MX_ALIGN)
-            kv_tiles[i] = kv_tile
-            k_pairs = kv_pool.tile([P, PAIR, HEADS * HEAD_DIM, PAIR], BF16, align_bytes=MX_ALIGN)
-            add_bias(k_pairs, kv_tile, accs, 0)
-            if i + 1 < SLABS:
-                x_mx[i + 1] = quantise_slab(x_mx_pool, x_grouped[i + 1])
-            for o in range(1, OUT_BLOCKS):
-                add_bias(k_pairs, kv_tile, accs, o)
-            if i >= 1:
-                quantise_kv_of_slab(i - 1)
-
+                state_of_column((i - 1) // HEIGHT_PASSES - 1)
+            add_bias(i, 0)
+            quantise_x(i + 1, 0, ROW_TILES)
+            for a in range(1, OUT_BLOCKS):
+                add_bias(i, a)
+            quantise_kv(i - 1, 0, OUT_BLOCKS)
             if i + LEAD < SLABS:
-                x_grouped[i + LEAD] = group_slab(nc.scalar.copy, transpose_slab(x_rows[i + LEAD]))
+                turn_x(i + LEAD, ALL)
+            relu_k(i)
 
-            relu_k(k_pairs, kv_tile)
-
-        quantise_kv_of_slab(SLABS - 1)
-        state_of_column(WIDTH - 1, kv_mx[WIDTH - 1][0], kv_mx[WIDTH - 1][1])
+        last = SLABS - 1
+        for a in range(OUT_BLOCKS):
+            project(last, a)
+        state_of_column(WIDTH - 2)
+        add_bias(last, 0)
+        add_bias(last, 1)
+        relu_k(last)
+        quantise_kv(last - 1, 0, OUT_BLOCKS)
+        add_bias(last, 2)
+        add_bias(last, 3)
+        quantise_kv(last, 0, HEADS)
+        quantise_kv(last, HEADS, HEADS)
+        state_of_column(WIDTH - 1)

@@ -58,8 +58,9 @@ def tile_linear_retention_pa_t_kernel(tc, x, Wk, bk, Wv, bv, out):
         nc.vector.memset(ones[:], 1.0)
         bias_row = const.tile([P, OUT_BLOCKS * HEAD_DIM], BF16)
         nc.vector.memset(bias_row[:], 0.0)
-        nc.scalar.dma_start(out=bias_row[0:1, 0 : HEADS * HEAD_DIM], in_=bk.unsqueeze(0))
-        nc.scalar.dma_start(out=bias_row[0:1, HEADS * HEAD_DIM : OUT_BLOCKS * HEAD_DIM], in_=bv.unsqueeze(0))
+        bias_in = const.tile([1, OUT_BLOCKS * HEAD_DIM], BF16)
+        nc.scalar.dma_start(out=bias_in[:, 0 : HEADS * HEAD_DIM], in_=bk.unsqueeze(0))
+        nc.scalar.dma_start(out=bias_in[:, HEADS * HEAD_DIM : OUT_BLOCKS * HEAD_DIM], in_=bv.unsqueeze(0))
         bias = const.tile([P, OUT_BLOCKS, HEAD_DIM], BF16)
 
         w_rows = {}
@@ -106,11 +107,13 @@ def tile_linear_retention_pa_t_kernel(tc, x, Wk, bk, Wv, bv, out):
                 nc.tensor.transpose(bank[:, f, :], rows[:].bitcast(F32)[:, f * P : (f + 1) * P], ident[:])
             nc.scalar.copy(out=words, in_=bank[:].rearrange("p (c u) m -> p c m u", u=PAIR))
 
-        def turn_weights(b):
+        def turn_weights(b, warm=0):
             for n in range(HEADS):
                 turn(w_rows[b][n], w_words[:, b, n])
+                if warm:
+                    keep_warm(warm)
 
-        def turn_x(i, ts):
+        def turn_x(i, ts, warm=0):
             if i not in x_grouped:
                 grouped = grouped_pool.tile([P, ROW_TILES * CHANNELS], BF16, name="grouped", align_bytes=MX_ALIGN)
                 x_grouped[i] = grouped
@@ -119,6 +122,8 @@ def tile_linear_retention_pa_t_kernel(tc, x, Wk, bk, Wv, bv, out):
             )
             for t in ts:
                 turn(x_rows[i][t], words[:, t])
+                if warm:
+                    keep_warm(warm)
 
         def quantise_weights(b):
             half = w_grouped[:].rearrange("p (b e) -> p b e", b=PAIR)
@@ -140,12 +145,20 @@ def tile_linear_retention_pa_t_kernel(tc, x, Wk, bk, Wv, bv, out):
                 in_=x_grouped[i][:, t0 * CHANNELS : (t0 + count) * CHANNELS],
             )
 
+        def load_bias_row():
+            nc.vector.tensor_copy(out=bias_row[0:1, :], in_=bias_in[:])
+
         def spread_bias():
             spread = flip_psum.tile([P, FLIPS, P], F32, tag="flip")
             nc.tensor.matmul(
                 out=spread[:].rearrange("p o j -> p (o j)"), lhsT=ones[:], rhs=bias_row[:], start=True, stop=True
             )
             nc.vector.tensor_copy(out=bias[:], in_=spread[:])
+
+        def keep_warm(count):
+            filler = proj_psum.tile([P, P], F32, tag="proj")
+            for j in range(count):
+                nc.tensor.matmul(out=filler[:], lhsT=ones[:], rhs=ones[:], start=True, stop=True)
 
         accs = {}
         k_pairs = {}
@@ -231,13 +244,16 @@ def tile_linear_retention_pa_t_kernel(tc, x, Wk, bk, Wv, bv, out):
 
         ALL = tuple(range(ROW_TILES))
 
-        turn_weights(0)
-        spread_bias()
+        keep_warm(20)
+        load_bias_row()
+        turn_weights(0, 2)
         quantise_weights(0)
-        turn_x(0, ALL)
+        turn_x(0, (0, 1), 2)
+        spread_bias()
+        turn_x(0, (2, 3))
         quantise_x(0, 0, 2)
-        project(0, 0)
         turn_weights(1)
+        project(0, 0)
         quantise_x(0, 2, 2)
         project(0, 1)
         add_bias(0, 0)

@@ -62,6 +62,7 @@ def tile_linear_retention_pa_t_kernel(tc, x, Wk, bk, Wv, bv, out):
         nc.scalar.dma_start(out=bias_in[:, 0 : HEADS * HEAD_DIM], in_=bk.unsqueeze(0))
         nc.scalar.dma_start(out=bias_in[:, HEADS * HEAD_DIM : OUT_BLOCKS * HEAD_DIM], in_=bv.unsqueeze(0))
         bias = const.tile([P, OUT_BLOCKS, HEAD_DIM], BF16)
+        bias_column = const.tile([P, HEADS], F32)
 
         w_rows = {}
         x_rows = {}
@@ -101,15 +102,18 @@ def tile_linear_retention_pa_t_kernel(tc, x, Wk, bk, Wv, bv, out):
         x_codes = {}
         x_scales = {}
 
-        def turn(rows, words):
+        def flip(rows):
             bank = flip_psum.tile([P, FLIPS, P], F32, tag="flip")
             for f in range(FLIPS):
                 nc.tensor.transpose(bank[:, f, :], rows[:].bitcast(F32)[:, f * P : (f + 1) * P], ident[:])
-            nc.scalar.copy(out=words, in_=bank[:].rearrange("p (c u) m -> p c m u", u=PAIR))
+            return bank
 
-        def turn_weights(b, warm=0):
+        def drain(copy, words, bank):
+            copy(out=words, in_=bank[:].rearrange("p (c u) m -> p c m u", u=PAIR))
+
+        def turn_weights(b, copy, warm=0):
             for n in range(HEADS):
-                turn(w_rows[b][n], w_words[:, b, n])
+                drain(copy, w_words[:, b, n], flip(w_rows[b][n]))
                 if warm:
                     keep_warm(warm)
 
@@ -121,7 +125,7 @@ def tile_linear_retention_pa_t_kernel(tc, x, Wk, bk, Wv, bv, out):
                 "p (r c m u) -> p r c m u", r=ROW_TILES, c=CHANNEL_PASSES, m=P, u=PAIR
             )
             for t in ts:
-                turn(x_rows[i][t], words[:, t])
+                drain(nc.scalar.copy, words[:, t], flip(x_rows[i][t]))
                 if warm:
                     keep_warm(warm)
 
@@ -154,6 +158,16 @@ def tile_linear_retention_pa_t_kernel(tc, x, Wk, bk, Wv, bv, out):
                 out=spread[:].rearrange("p o j -> p (o j)"), lhsT=ones[:], rhs=bias_row[:], start=True, stop=True
             )
             nc.vector.tensor_copy(out=bias[:], in_=spread[:])
+            column = flip_psum.tile([P, HEADS], F32, tag="flip")
+            for n in range(HEADS):
+                nc.tensor.matmul(
+                    out=column[:, n : n + 1],
+                    lhsT=bias_row[:, n * HEAD_DIM : (n + 1) * HEAD_DIM],
+                    rhs=ones[:, 0:1],
+                    start=True,
+                    stop=True,
+                )
+            nc.vector.tensor_copy(out=bias_column[:], in_=column[:])
 
         def keep_warm(count):
             filler = proj_psum.tile([P, P], F32, tag="proj")
@@ -162,6 +176,7 @@ def tile_linear_retention_pa_t_kernel(tc, x, Wk, bk, Wv, bv, out):
 
         accs = {}
         k_pairs = {}
+        k_turned = {}
         kv_tiles = {}
         kv_mx = {}
 
@@ -184,6 +199,49 @@ def tile_linear_retention_pa_t_kernel(tc, x, Wk, bk, Wv, bv, out):
                         stop=(c == CHANNEL_PASSES - 1),
                     )
             accs[i, a] = acc
+
+        def project_turned(i, n):
+            acc = proj_psum.tile([P, PACK, P], F32, tag="proj")
+            for t in range(PACK):
+                for c in range(CHANNEL_PASSES):
+                    nc.tensor.matmul_mx(
+                        out=acc[:, t, :],
+                        lhsT=w_codes[:, 0, c, n * P : (n + 1) * P].bitcast(FP8X4),
+                        lhsT_scale=w_scales[:, 0, c, n * P : (n + 1) * P],
+                        rhs=x_codes[i][:, t, c, :].bitcast(FP8X4),
+                        rhs_scale=x_scales[i][:, t, c, :],
+                        start=(c == 0),
+                        stop=(c == CHANNEL_PASSES - 1),
+                    )
+            accs[i, n] = acc
+
+        def relu_turned(i, n):
+            if n == 0:
+                turned = kv_pool.tile([P, HEADS, PAIR, P, PAIR], BF16, align_bytes=MX_ALIGN)
+                kv_tile = kv_pool.tile([P, OUT_BLOCKS, HEAD_DIM, PACK], BF16, align_bytes=MX_ALIGN)
+                k_turned[i] = turned
+                kv_tiles[i] = kv_tile
+            nc.scalar.activation(
+                out=k_turned[i][:, n],
+                in_=accs[i, n][:].rearrange("p (u e) m -> p u m e", u=PAIR),
+                func=mybir.ActivationFunctionType.Relu,
+                bias=bias_column[:, n : n + 1],
+            )
+
+        def turn_back(i, copy):
+            bank = flip_psum.tile([P, HEADS, PAIR, P], F32, tag="flip")
+            words = k_turned[i][:].rearrange("p n u m e -> p (n u m e)").bitcast(F32)
+            for f in range(HEADS * PAIR):
+                nc.tensor.transpose(
+                    bank[:].rearrange("p n u d -> p (n u) d")[:, f, :], words[:, f * P : (f + 1) * P], ident[:]
+                )
+            copy(
+                out=kv_tiles[i][:, 0:HEADS]
+                .rearrange("p n j t -> p (n j t)")
+                .bitcast(F32)
+                .rearrange("p (n j u) -> p n j u", n=HEADS, u=PAIR),
+                in_=bank[:].rearrange("p n u d -> p n d u"),
+            )
 
         def add_bias(i, a):
             if a == 0:
@@ -246,13 +304,13 @@ def tile_linear_retention_pa_t_kernel(tc, x, Wk, bk, Wv, bv, out):
 
         keep_warm(20)
         load_bias_row()
-        turn_weights(0, 2)
+        turn_weights(0, nc.scalar.copy, 2)
         quantise_weights(0)
         turn_x(0, (0, 1), 2)
         spread_bias()
         turn_x(0, (2, 3))
         quantise_x(0, 0, 2)
-        turn_weights(1)
+        turn_weights(1, nc.scalar.copy)
         project(0, 0)
         quantise_x(0, 2, 2)
         project(0, 1)
@@ -266,23 +324,22 @@ def tile_linear_retention_pa_t_kernel(tc, x, Wk, bk, Wv, bv, out):
         add_bias(0, 2)
         quantise_x(1, 2, 2)
         add_bias(0, 3)
-        project(1, 0)
         turn_x(2, ALL)
         relu_k(0)
+        project(1, 0)
         project(1, 1)
-        add_bias(1, 0)
-        quantise_x(2, 0, 2)
-        add_bias(1, 1)
-        quantise_x(2, 2, 2)
         project(1, 2)
         project(1, 3)
+        add_bias(1, 0)
+        add_bias(1, 1)
+        quantise_x(2, 0, ROW_TILES)
         add_bias(1, 2)
         add_bias(1, 3)
         quantise_kv(0, 0, OUT_BLOCKS)
         turn_x(3, ALL)
         relu_k(1)
 
-        for i in range(2, SLABS - 1):
+        for i in range(2, SLABS - 2):
             for a in range(OUT_BLOCKS):
                 project(i, a)
             if i > HEIGHT_PASSES and (i - 1) % HEIGHT_PASSES == 0:
@@ -297,15 +354,27 @@ def tile_linear_retention_pa_t_kernel(tc, x, Wk, bk, Wv, bv, out):
             relu_k(i)
 
         last = SLABS - 1
+        i = last - 1
         for a in range(OUT_BLOCKS):
-            project(last, a)
+            project(i, a)
+        add_bias(i, 0)
+        quantise_x(last, 0, ROW_TILES)
+        add_bias(i, 1)
+        add_bias(i, 2)
+        add_bias(i, 3)
+        relu_k(i)
+        quantise_kv(i - 1, 0, OUT_BLOCKS)
+        i = last
+        for n in range(HEADS):
+            project_turned(i, n)
+            relu_turned(i, n)
+        for a in (2, 3):
+            project(i, a)
         state_of_column(WIDTH - 2)
-        add_bias(last, 0)
-        add_bias(last, 1)
-        relu_k(last)
-        quantise_kv(last - 1, 0, OUT_BLOCKS)
-        add_bias(last, 2)
-        add_bias(last, 3)
-        quantise_kv(last, 0, HEADS)
+        quantise_kv(i - 1, 0, OUT_BLOCKS)
+        add_bias(i, 2)
+        add_bias(i, 3)
+        turn_back(i, nc.scalar.copy)
         quantise_kv(last, HEADS, HEADS)
+        quantise_kv(last, 0, HEADS)
         state_of_column(WIDTH - 1)

@@ -62,7 +62,7 @@ def tile_linear_retention_pa_t_kernel(tc, x, Wk, bk, Wv, bv, out):
         nc.scalar.dma_start(out=bias_in[:, 0 : HEADS * HEAD_DIM], in_=bk.unsqueeze(0))
         nc.scalar.dma_start(out=bias_in[:, HEADS * HEAD_DIM : OUT_BLOCKS * HEAD_DIM], in_=bv.unsqueeze(0))
         bias = const.tile([P, OUT_BLOCKS, HEAD_DIM], BF16)
-        bias_column = const.tile([P, HEADS], F32)
+        bias_column = const.tile([P, MX_ALIGN], F32)
 
         w_rows = {}
         x_rows = {}
@@ -158,6 +158,8 @@ def tile_linear_retention_pa_t_kernel(tc, x, Wk, bk, Wv, bv, out):
                 out=spread[:].rearrange("p o j -> p (o j)"), lhsT=ones[:], rhs=bias_row[:], start=True, stop=True
             )
             nc.vector.tensor_copy(out=bias[:], in_=spread[:])
+
+        def spread_column():
             column = flip_psum.tile([P, HEADS], F32, tag="flip")
             for n in range(HEADS):
                 nc.tensor.matmul(
@@ -167,7 +169,7 @@ def tile_linear_retention_pa_t_kernel(tc, x, Wk, bk, Wv, bv, out):
                     start=True,
                     stop=True,
                 )
-            nc.vector.tensor_copy(out=bias_column[:], in_=column[:])
+            nc.scalar.copy(out=bias_column[:, 0:HEADS], in_=column[:])
 
         def keep_warm(count):
             filler = proj_psum.tile([P, P], F32, tag="proj")
@@ -324,15 +326,16 @@ def tile_linear_retention_pa_t_kernel(tc, x, Wk, bk, Wv, bv, out):
         add_bias(0, 2)
         quantise_x(1, 2, 2)
         add_bias(0, 3)
+        project(1, 0)
         turn_x(2, ALL)
         relu_k(0)
-        project(1, 0)
         project(1, 1)
+        add_bias(1, 0)
+        quantise_x(2, 0, 2)
+        add_bias(1, 1)
+        quantise_x(2, 2, 2)
         project(1, 2)
         project(1, 3)
-        add_bias(1, 0)
-        add_bias(1, 1)
-        quantise_x(2, 0, ROW_TILES)
         add_bias(1, 2)
         add_bias(1, 3)
         quantise_kv(0, 0, OUT_BLOCKS)
@@ -342,21 +345,23 @@ def tile_linear_retention_pa_t_kernel(tc, x, Wk, bk, Wv, bv, out):
         for i in range(2, SLABS - 2):
             for a in range(OUT_BLOCKS):
                 project(i, a)
-            if i > HEIGHT_PASSES and (i - 1) % HEIGHT_PASSES == 0:
-                state_of_column((i - 1) // HEIGHT_PASSES - 1)
             add_bias(i, 0)
+            add_bias(i, 1)
             quantise_x(i + 1, 0, ROW_TILES)
-            for a in range(1, OUT_BLOCKS):
-                add_bias(i, a)
+            add_bias(i, 2)
+            add_bias(i, 3)
             quantise_kv(i - 1, 0, OUT_BLOCKS)
             if i + LEAD < SLABS:
                 turn_x(i + LEAD, ALL)
             relu_k(i)
+            if i > HEIGHT_PASSES and (i - 1) % HEIGHT_PASSES == 0:
+                state_of_column((i - 1) // HEIGHT_PASSES - 1)
 
         last = SLABS - 1
         i = last - 1
         for a in range(OUT_BLOCKS):
             project(i, a)
+        spread_column()
         add_bias(i, 0)
         quantise_x(last, 0, ROW_TILES)
         add_bias(i, 1)

@@ -230,19 +230,17 @@ def tile_linear_retention_pa_t_kernel(tc, x, Wk, bk, Wv, bv, out):
                 bias=bias_column[:, n : n + 1],
             )
 
-        def turn_back(i, copy):
-            bank = flip_psum.tile([P, HEADS, PAIR, P], F32, tag="flip")
-            words = k_turned[i][:].rearrange("p n u m e -> p (n u m e)").bitcast(F32)
-            for f in range(HEADS * PAIR):
-                nc.tensor.transpose(
-                    bank[:].rearrange("p n u d -> p (n u) d")[:, f, :], words[:, f * P : (f + 1) * P], ident[:]
-                )
-            copy(
-                out=kv_tiles[i][:, 0:HEADS]
-                .rearrange("p n j t -> p (n j t)")
+        def turn_back(i, n):
+            bank = flip_psum.tile([P, PAIR, P], F32, tag="flip")
+            words = k_turned[i][:, n].rearrange("p u m e -> p (u m e)").bitcast(F32)
+            for u in range(PAIR):
+                nc.tensor.transpose(bank[:, u, :], words[:, u * P : (u + 1) * P], ident[:])
+            nc.scalar.copy(
+                out=kv_tiles[i][:, n]
+                .rearrange("p j t -> p (j t)")
                 .bitcast(F32)
-                .rearrange("p (n j u) -> p n j u", n=HEADS, u=PAIR),
-                in_=bank[:].rearrange("p n u d -> p n d u"),
+                .rearrange("p (j u) -> p j u", u=PAIR),
+                in_=bank[:].rearrange("p u d -> p d u"),
             )
 
         def add_bias(i, a):
@@ -284,6 +282,22 @@ def tile_linear_retention_pa_t_kernel(tc, x, Wk, bk, Wv, bv, out):
                 scales=kv_mx[w][1][:, g, o0 : o0 + count].rearrange("p o j -> p (o j)"),
                 in_=kv_tiles[i][:, o0 : o0 + count].rearrange("p o j t -> p (o j t)"),
             )
+
+        def state_of_head(w, n):
+            kv_codes, kv_scales = kv_mx[w]
+            state = flip_psum.tile([P, P], F32, tag="flip")
+            for g in range(HEIGHT_PASSES):
+                nc.tensor.matmul_mx(
+                    out=state[:],
+                    lhsT=kv_codes[:, g, n, :].bitcast(FP8X4),
+                    lhsT_scale=kv_scales[:, g, n, :],
+                    rhs=kv_codes[:, g, HEADS + n, :].bitcast(FP8X4),
+                    rhs_scale=kv_scales[:, g, HEADS + n, :],
+                    start=(g == 0),
+                    stop=(g == HEIGHT_PASSES - 1),
+                )
+            nc.scalar.copy(out=out_sb[:, w, n], in_=state[:])
+            nc.sync.dma_start(out=out_columns[w][:, n], in_=out_sb[:, w, n])
 
         def state_of_column(w):
             kv_codes, kv_scales = kv_mx[w]
@@ -363,8 +377,9 @@ def tile_linear_retention_pa_t_kernel(tc, x, Wk, bk, Wv, bv, out):
             project(i, a)
         spread_column()
         add_bias(i, 0)
-        quantise_x(last, 0, ROW_TILES)
+        quantise_x(last, 0, 2)
         add_bias(i, 1)
+        quantise_x(last, 2, 2)
         add_bias(i, 2)
         add_bias(i, 3)
         relu_k(i)
@@ -375,11 +390,14 @@ def tile_linear_retention_pa_t_kernel(tc, x, Wk, bk, Wv, bv, out):
             relu_turned(i, n)
         for a in (2, 3):
             project(i, a)
-        state_of_column(WIDTH - 2)
         quantise_kv(i - 1, 0, OUT_BLOCKS)
         add_bias(i, 2)
         add_bias(i, 3)
-        turn_back(i, nc.scalar.copy)
+        for n in range(HEADS):
+            turn_back(i, n)
+        state_of_column(WIDTH - 2)
         quantise_kv(last, HEADS, HEADS)
-        quantise_kv(last, 0, HEADS)
-        state_of_column(WIDTH - 1)
+        for n in range(HEADS):
+            quantise_kv(last, n, 1)
+        for n in range(HEADS):
+            state_of_head(WIDTH - 1, n)

from contextlib import ExitStack

import concourse.mybir as mybir
from concourse.masks import make_identity

BF16 = mybir.dt.bfloat16
F32 = mybir.dt.float32
U32 = mybir.dt.uint32
U8 = mybir.dt.uint8
FP8X4 = mybir.dt.float8_e4m3fn_x4

P = 128
PACK = 4
K_PASS = P * PACK
MX_ALIGN = 64

HEIGHT = 1024
WIDTH = 8
CHANNELS = 1024
HEADS = 2
HEAD_DIM = 128

ROW_TILES = 4
CHANNEL_PASSES = CHANNELS // K_PASS
HEIGHT_PASSES = HEIGHT // K_PASS
SLABS = WIDTH * HEIGHT_PASSES
OUT_BLOCKS = 2 * HEADS
PAIR = 2
WORDS = CHANNELS // PAIR
FLIPS = WORDS // P
LEAD = 2
FLIP_BANKS = ROW_TILES
SPARE = 1

FLOPS = 2 * HEIGHT * WIDTH * CHANNELS * OUT_BLOCKS * HEAD_DIM + 2 * WIDTH * HEADS * HEIGHT * HEAD_DIM * HEAD_DIM


def tile_linear_retention_pa_t_kernel(tc, x, Wk, bk, Wv, bv, out):
    nc = tc.nc

    x_slabs = x.rearrange("b (g p t) w a -> (b g) w p t a", g=HEIGHT_PASSES, p=P, t=PACK)
    out_columns = out.rearrange("b w n d e -> (b w) d n e")

    with ExitStack() as ctx:
        ctx.enter_context(tc.manual_schedule())
        const = ctx.enter_context(tc.tile_pool(name="const", bufs=1))
        rows_pool = ctx.enter_context(tc.tile_pool(name="rows", bufs=SLABS * ROW_TILES))
        grouped_pool = ctx.enter_context(tc.tile_pool(name="grouped", bufs=LEAD + 1))
        x_mx_pool = ctx.enter_context(tc.tile_pool(name="x_mx", bufs=2 + SPARE))
        kv_pool = ctx.enter_context(tc.tile_pool(name="kv", bufs=2 + SPARE))
        flip_psum = ctx.enter_context(tc.psum_pool(name="flip_psum", bufs=FLIP_BANKS))
        proj_psum = ctx.enter_context(tc.psum_pool(name="proj_psum", bufs=OUT_BLOCKS))

        ident = const.tile([P, P], F32)
        make_identity(nc, ident[:])

        ones = const.tile([P, P], BF16)
        nc.vector.memset(ones[:], 1.0)
        bias_row = const.tile([P, OUT_BLOCKS * HEAD_DIM], BF16)
        nc.vector.memset(bias_row[:], 0.0)
        bias_in = const.tile([1, OUT_BLOCKS * HEAD_DIM], BF16)
        nc.scalar.dma_start(out=bias_in[:, 0 : HEADS * HEAD_DIM], in_=bk.unsqueeze(0))
        nc.scalar.dma_start(out=bias_in[:, HEADS * HEAD_DIM : OUT_BLOCKS * HEAD_DIM], in_=bv.unsqueeze(0))
        bias = const.tile([P, OUT_BLOCKS, HEAD_DIM], BF16)
        bias_column = const.tile([P, MX_ALIGN], F32)

        w_rows = {}
        x_rows = {}

        def load_weights(b, weights):
            w_rows[b] = []
            for n in range(HEADS):
                rows = const.tile([P, CHANNELS], BF16, name="w_rows%d_%d" % (b, n))
                nc.sync.dma_start(out=rows[:], in_=weights[n * HEAD_DIM : (n + 1) * HEAD_DIM, :])
                w_rows[b].append(rows)

        def load_slab(i):
            w, g = divmod(i, HEIGHT_PASSES)
            x_rows[i] = []
            for t in range(ROW_TILES):
                rows = rows_pool.tile([P, CHANNELS], BF16)
                nc.sync.dma_start(out=rows[:], in_=x_slabs[g, w][:, t, :])
                x_rows[i].append(rows)

        load_weights(0, Wk)
        load_slab(0)
        load_weights(1, Wv)
        for i in range(1, SLABS):
            load_slab(i)

        out_sb = const.tile([P, WIDTH, HEADS, HEAD_DIM], F32)

        w_grouped = grouped_pool.tile([P, ROW_TILES * CHANNELS], BF16, name="grouped", align_bytes=MX_ALIGN)
        w_words = (
            w_grouped[:]
            .bitcast(F32)
            .rearrange("p (b c n m u) -> p b n c m u", b=PAIR, c=CHANNEL_PASSES, n=HEADS, m=P, u=PAIR)
        )
        w_codes = const.tile([P, PAIR, CHANNEL_PASSES, HEADS * P], U32, align_bytes=MX_ALIGN)
        w_scales = const.tile([P, PAIR, CHANNEL_PASSES, HEADS * P], U8, align_bytes=MX_ALIGN)
        x_grouped = {}
        x_codes = {}
        x_scales = {}

        def flip(rows):
            bank = flip_psum.tile([P, FLIPS, P], F32, tag="flip")
            for f in range(FLIPS):
                nc.tensor.transpose(bank[:, f, :], rows[:].bitcast(F32)[:, f * P : (f + 1) * P], ident[:])
            return bank

        def drain(copy, words, bank):
            copy(out=words, in_=bank[:].rearrange("p (c u) m -> p c m u", u=PAIR))

        def turn_weights(b, copy, warm=0):
            for n in range(HEADS):
                drain(copy, w_words[:, b, n], flip(w_rows[b][n]))
                if warm:
                    keep_warm(warm)

        def turn_x(i, ts, warm=0):
            if i not in x_grouped:
                grouped = grouped_pool.tile([P, ROW_TILES * CHANNELS], BF16, name="grouped", align_bytes=MX_ALIGN)
                x_grouped[i] = grouped
            words = x_grouped[i][:].bitcast(F32).rearrange(
                "p (r c m u) -> p r c m u", r=ROW_TILES, c=CHANNEL_PASSES, m=P, u=PAIR
            )
            for t in ts:
                drain(nc.scalar.copy, words[:, t], flip(x_rows[i][t]))
                if warm:
                    keep_warm(warm)

        def quantise_weights(b):
            half = w_grouped[:].rearrange("p (b e) -> p b e", b=PAIR)
            nc.vector.quantize_mx(
                out=w_codes[:, b].rearrange("p c j -> p (c j)").bitcast(FP8X4),
                scales=w_scales[:, b].rearrange("p c j -> p (c j)"),
                in_=half[:, b],
            )

        def quantise_x(i, t0, count):
            if i not in x_codes:
                codes = x_mx_pool.tile([P, ROW_TILES, CHANNEL_PASSES, P], U32, align_bytes=MX_ALIGN)
                scales = x_mx_pool.tile([P, ROW_TILES, CHANNEL_PASSES, P], U8, align_bytes=MX_ALIGN)
                x_codes[i] = codes
                x_scales[i] = scales
            nc.vector.quantize_mx(
                out=x_codes[i][:, t0 : t0 + count].rearrange("p r c m -> p (r c m)").bitcast(FP8X4),
                scales=x_scales[i][:, t0 : t0 + count].rearrange("p r c m -> p (r c m)"),
                in_=x_grouped[i][:, t0 * CHANNELS : (t0 + count) * CHANNELS],
            )

        def load_bias_row():
            nc.vector.tensor_copy(out=bias_row[0:1, :], in_=bias_in[:])

        def spread_bias():
            spread = flip_psum.tile([P, FLIPS, P], F32, tag="flip")
            nc.tensor.matmul(
                out=spread[:].rearrange("p o j -> p (o j)"), lhsT=ones[:], rhs=bias_row[:], start=True, stop=True
            )
            nc.vector.tensor_copy(out=bias[:], in_=spread[:])

        def spread_column():
            column = flip_psum.tile([P, HEADS], F32, tag="flip")
            for n in range(HEADS):
                nc.tensor.matmul(
                    out=column[:, n : n + 1],
                    lhsT=bias_row[:, n * HEAD_DIM : (n + 1) * HEAD_DIM],
                    rhs=ones[:, 0:1],
                    start=True,
                    stop=True,
                )
            nc.scalar.copy(out=bias_column[:, 0:HEADS], in_=column[:])

        def keep_warm(count):
            filler = proj_psum.tile([P, P], F32, tag="proj")
            for j in range(count):
                nc.tensor.matmul(out=filler[:], lhsT=ones[:], rhs=ones[:], start=True, stop=True)

        accs = {}
        k_pairs = {}
        k_turned = {}
        kv_tiles = {}
        kv_mx = {}

        def project(i, a):
            is_k = a < HEADS
            ts = (PAIR * a, PAIR * a + 1) if is_k else tuple(range(PACK))
            width = HEADS * HEAD_DIM if is_k else HEAD_DIM
            lo = 0 if is_k else (a - HEADS) * HEAD_DIM
            b = 0 if is_k else 1
            acc = proj_psum.tile([P, len(ts), width], F32, tag="proj")
            for at, t in enumerate(ts):
                for c in range(CHANNEL_PASSES):
                    nc.tensor.matmul_mx(
                        out=acc[:, at, :],
                        lhsT=x_codes[i][:, t, c, :].bitcast(FP8X4),
                        lhsT_scale=x_scales[i][:, t, c, :],
                        rhs=w_codes[:, b, c, lo : lo + width].bitcast(FP8X4),
                        rhs_scale=w_scales[:, b, c, lo : lo + width],
                        start=(c == 0),
                        stop=(c == CHANNEL_PASSES - 1),
                    )
            accs[i, a] = acc

        def project_turned(i, n):
            acc = proj_psum.tile([P, PACK, P], F32, tag="proj")
            for t in range(PACK):
                for c in range(CHANNEL_PASSES):
                    nc.tensor.matmul_mx(
                        out=acc[:, t, :],
                        lhsT=w_codes[:, 0, c, n * P : (n + 1) * P].bitcast(FP8X4),
                        lhsT_scale=w_scales[:, 0, c, n * P : (n + 1) * P],
                        rhs=x_codes[i][:, t, c, :].bitcast(FP8X4),
                        rhs_scale=x_scales[i][:, t, c, :],
                        start=(c == 0),
                        stop=(c == CHANNEL_PASSES - 1),
                    )
            accs[i, n] = acc

        def relu_turned(i, n):
            if n == 0:
                turned = kv_pool.tile([P, HEADS, PAIR, P, PAIR], BF16, align_bytes=MX_ALIGN)
                kv_tile = kv_pool.tile([P, OUT_BLOCKS, HEAD_DIM, PACK], BF16, align_bytes=MX_ALIGN)
                k_turned[i] = turned
                kv_tiles[i] = kv_tile
            nc.scalar.activation(
                out=k_turned[i][:, n],
                in_=accs[i, n][:].rearrange("p (u e) m -> p u m e", u=PAIR),
                func=mybir.ActivationFunctionType.Relu,
                bias=bias_column[:, n : n + 1],
            )

        def turn_back(i, n):
            bank = flip_psum.tile([P, PAIR, P], F32, tag="flip")
            words = k_turned[i][:, n].rearrange("p u m e -> p (u m e)").bitcast(F32)
            for u in range(PAIR):
                nc.tensor.transpose(bank[:, u, :], words[:, u * P : (u + 1) * P], ident[:])
            nc.scalar.copy(
                out=kv_tiles[i][:, n]
                .rearrange("p j t -> p (j t)")
                .bitcast(F32)
                .rearrange("p (j u) -> p j u", u=PAIR),
                in_=bank[:].rearrange("p u d -> p d u"),
            )

        def add_bias(i, a):
            if a == 0:
                pairs = kv_pool.tile([P, PAIR, HEADS * HEAD_DIM, PAIR], BF16, align_bytes=MX_ALIGN)
                kv_tile = kv_pool.tile([P, OUT_BLOCKS, HEAD_DIM, PACK], BF16, align_bytes=MX_ALIGN)
                k_pairs[i] = pairs
                kv_tiles[i] = kv_tile
            if a < HEADS:
                dest = k_pairs[i][:, a]
                channels = bias[:, 0:HEADS].rearrange("p n j -> p (n j)")
            else:
                dest = kv_tiles[i][:, a]
                channels = bias[:, a]
            heights = PAIR if a < HEADS else PACK
            width = HEADS * HEAD_DIM if a < HEADS else HEAD_DIM
            nc.vector.tensor_tensor(
                out=dest,
                in0=accs[i, a][:].rearrange("p t j -> p j t"),
                in1=channels.unsqueeze(2).to_broadcast([P, width, heights]),
                op=mybir.AluOpType.add,
            )

        def relu_k(i):
            nc.scalar.activation(
                out=kv_tiles[i][:, 0:HEADS].rearrange("p n j (a e) -> p (n j) a e", a=PAIR),
                in_=k_pairs[i][:].rearrange("p a j e -> p j a e"),
                func=mybir.ActivationFunctionType.Relu,
            )

        def quantise_kv(i, o0, count):
            w, g = divmod(i, HEIGHT_PASSES)
            if w not in kv_mx:
                kv_codes = kv_pool.tile([P, HEIGHT_PASSES, OUT_BLOCKS, HEAD_DIM], U32, align_bytes=MX_ALIGN)
                kv_scales = kv_pool.tile([P, HEIGHT_PASSES, OUT_BLOCKS, HEAD_DIM], U8, align_bytes=MX_ALIGN)
                kv_mx[w] = (kv_codes, kv_scales)
            nc.vector.quantize_mx(
                out=kv_mx[w][0][:, g, o0 : o0 + count].rearrange("p o j -> p (o j)").bitcast(FP8X4),
                scales=kv_mx[w][1][:, g, o0 : o0 + count].rearrange("p o j -> p (o j)"),
                in_=kv_tiles[i][:, o0 : o0 + count].rearrange("p o j t -> p (o j t)"),
            )

        def state_of_head(w, n):
            kv_codes, kv_scales = kv_mx[w]
            state = flip_psum.tile([P, P], F32, tag="flip")
            for g in range(HEIGHT_PASSES):
                nc.tensor.matmul_mx(
                    out=state[:],
                    lhsT=kv_codes[:, g, n, :].bitcast(FP8X4),
                    lhsT_scale=kv_scales[:, g, n, :],
                    rhs=kv_codes[:, g, HEADS + n, :].bitcast(FP8X4),
                    rhs_scale=kv_scales[:, g, HEADS + n, :],
                    start=(g == 0),
                    stop=(g == HEIGHT_PASSES - 1),
                )
            nc.scalar.copy(out=out_sb[:, w, n], in_=state[:])
            nc.sync.dma_start(out=out_columns[w][:, n], in_=out_sb[:, w, n])

        def state_of_column(w):
            kv_codes, kv_scales = kv_mx[w]
            state = flip_psum.tile([P, FLIPS, P], F32, tag="flip")
            for n in range(HEADS):
                for g in range(HEIGHT_PASSES):
                    nc.tensor.matmul_mx(
                        out=state[:, n, :],
                        lhsT=kv_codes[:, g, n, :].bitcast(FP8X4),
                        lhsT_scale=kv_scales[:, g, n, :],
                        rhs=kv_codes[:, g, HEADS + n, :].bitcast(FP8X4),
                        rhs_scale=kv_scales[:, g, HEADS + n, :],
                        start=(g == 0),
                        stop=(g == HEIGHT_PASSES - 1),
                    )
            nc.scalar.copy(out=out_sb[:, w], in_=state[:, 0:HEADS, :])
            nc.sync.dma_start(out=out_columns[w], in_=out_sb[:, w])

        ALL = tuple(range(ROW_TILES))

        keep_warm(20)
        load_bias_row()
        turn_weights(0, nc.scalar.copy, 2)
        quantise_weights(0)
        turn_x(0, (0, 1), 2)
        spread_bias()
        turn_x(0, (2, 3))
        quantise_x(0, 0, 2)
        turn_weights(1, nc.scalar.copy)
        project(0, 0)
        quantise_x(0, 2, 2)
        project(0, 1)
        add_bias(0, 0)
        quantise_weights(1)
        turn_x(1, ALL)
        add_bias(0, 1)
        project(0, 2)
        project(0, 3)
        quantise_x(1, 0, 2)
        add_bias(0, 2)
        quantise_x(1, 2, 2)
        add_bias(0, 3)
        project(1, 0)
        turn_x(2, ALL)
        relu_k(0)
        project(1, 1)
        add_bias(1, 0)
        quantise_x(2, 0, 2)
        add_bias(1, 1)
        quantise_x(2, 2, 2)
        project(1, 2)
        project(1, 3)
        add_bias(1, 2)
        add_bias(1, 3)
        quantise_kv(0, 0, OUT_BLOCKS)
        turn_x(3, ALL)
        relu_k(1)

        for i in range(2, SLABS - 2):
            for a in range(OUT_BLOCKS):
                project(i, a)
            add_bias(i, 0)
            add_bias(i, 1)
            quantise_x(i + 1, 0, ROW_TILES)
            add_bias(i, 2)
            add_bias(i, 3)
            quantise_kv(i - 1, 0, OUT_BLOCKS)
            if i + LEAD < SLABS:
                turn_x(i + LEAD, ALL)
            relu_k(i)
            if i > HEIGHT_PASSES and (i - 1) % HEIGHT_PASSES == 0:
                state_of_column((i - 1) // HEIGHT_PASSES - 1)

        last = SLABS - 1
        i = last - 1
        for a in range(OUT_BLOCKS):
            project(i, a)
        spread_column()
        add_bias(i, 0)
        quantise_x(last, 0, 2)
        add_bias(i, 1)
        quantise_x(last, 2, 2)
        add_bias(i, 2)
        add_bias(i, 3)
        relu_k(i)
        quantise_kv(i - 1, 0, OUT_BLOCKS)
        i = last
        for n in range(HEADS):
            project_turned(i, n)
            relu_turned(i, n)
        for a in (2, 3):
            project(i, a)
        quantise_kv(i - 1, 0, OUT_BLOCKS)
        add_bias(i, 2)
        add_bias(i, 3)
        for n in range(HEADS):
            turn_back(i, n)
        state_of_column(WIDTH - 2)
        quantise_kv(last, HEADS, HEADS)
        for n in range(HEADS):
            quantise_kv(last, n, 1)
        for n in range(HEADS):
            state_of_head(WIDTH - 1, n)
